import numpy as np
import ml_dtypes


def mxq(x, axis, fmt="e4m3"):
    dtype, down = {"e4m3": (ml_dtypes.float8_e4m3fn, 7), "e5m2": (ml_dtypes.float8_e5m2, 14)}[fmt]
    v = np.moveaxis(np.asarray(x, np.float32).astype(ml_dtypes.bfloat16).astype(np.float64), axis, -1)
    blocks = v.reshape(v.shape[:-1] + (-1, 32))
    amax = np.abs(blocks).max(-1, keepdims=True)
    byte = np.maximum(np.where(amax > 0, np.frexp(amax)[1] - 1 + 127, 0) - down, 1)
    scale = np.exp2(byte - 127.0)
    codes = (blocks / scale).astype(np.float32).astype(dtype).astype(np.float64)
    return np.moveaxis((codes * scale).reshape(v.shape), -1, axis)


WIDE = False


def mx_kscale(k):
    if not WIDE:
        return np.ones(k)
    levels = np.array([10, -10, 5, -5, 0])
    a = np.random.permutation(np.resize(levels, k // 512 * 4)).reshape(k // 512, 4)
    idx = np.arange(k)
    return np.exp2(a[idx // 512, idx % 128 // 32])


BF16 = ml_dtypes.bfloat16


def bf(x):
    return np.asarray(x, np.float32).astype(BF16)


def f64(x):
    return np.asarray(x).astype(np.float64)


B, R, U, HID, G = 1024, 1024, 512, 1024, 1024


def sigmoid(v):
    return 1.0 / (1.0 + np.exp(-v))


def setup_inputs():
    s = mx_kscale(R)
    return {"y_tilde": bf(np.random.standard_normal((B, R)) * s),
            "z_next": bf(np.random.standard_normal((B, R)) * s),
            "dt": bf(0.3 + 0.2 * np.random.random(1)),
            "glu_w1": bf(np.random.standard_normal((G, R)) * 1.5 / np.sqrt(R) / s),
            "glu_w2": bf(np.random.standard_normal((G, R)) / np.sqrt(R) / s),
            "glu_b1": bf(np.random.standard_normal(G) * 0.3),
            "glu_b2": bf(np.random.standard_normal(G) * 0.3)}


def reference(y_tilde, z_next, dt, glu_w1, glu_w2, glu_b1, glu_b2):
    y_next = f64(y_tilde) + f64(dt) * f64(z_next)
    yq = mxq(y_next, 1, "e4m3")
    gate = sigmoid((yq @ mxq(f64(glu_w1), 1, "e4m3").T) + f64(glu_b1))
    return gate * ((yq @ mxq(f64(glu_w2), 1, "e4m3").T) + f64(glu_b2))

@@ -1,0 +1,280 @@
+from contextlib import ExitStack
+
+import concourse.mybir as mybir
+from concourse.masks import make_identity
+
+F32 = mybir.dt.float32
+BF16 = mybir.dt.bfloat16
+U32 = mybir.dt.uint32
+U8 = mybir.dt.uint8
+FP8X4 = mybir.dt.float8_e4m3fn_x4
+ALU = mybir.AluOpType
+ACT = mybir.ActivationFunctionType
+
+P = 128
+ROWS = 1024
+K = 1024
+UNITS = 1024
+PACK = 4
+PASSES = K // (P * PACK)
+ROW_TILES = ROWS // P
+UNIT_TILES = UNITS // P
+CHUNK_TILES = 4
+CHUNK = CHUNK_TILES * P
+CHUNKS = ROW_TILES // CHUNK_TILES
+STEPS = CHUNKS * UNIT_TILES
+STORE_TILES = 2
+
+FLOPS = 2 * 2 * ROWS * K * UNITS
+
+
+def tile_instrumentedlocmblock_pb_kernel(
+    tc, y_tilde, z_next, dt, glu_w1, glu_w2, glu_b1, glu_b2, out
+):
+    nc = tc.nc
+    with ExitStack() as ctx:
+        ctx.enter_context(tc.manual_schedule())
+        keep = ctx.enter_context(tc.tile_pool(name="keep", bufs=1))
+        rows_pool = ctx.enter_context(tc.tile_pool(name="rows", bufs=4))
+        grouped_pool = ctx.enter_context(tc.tile_pool(name="grouped", bufs=4))
+        gated_pool = ctx.enter_context(tc.tile_pool(name="gated", bufs=3))
+        acc_pool = ctx.enter_context(tc.psum_pool(name="acc", bufs=2))
+        flip_in_pool = ctx.enter_context(tc.psum_pool(name="flip_in", bufs=2))
+        flip_out_pool = ctx.enter_context(tc.psum_pool(name="flip_out", bufs=2))
+
+        dt_bf16 = keep.tile([P, 1], BF16)
+        nc.scalar.dma_start(out=dt_bf16[:], in_=dt.partition_broadcast(P))
+
+        bias_rows = keep.tile([P, P], BF16)
+        nc.vector.memset(bias_rows[:], 0.0)
+        nc.scalar.dma_start(
+            out=bias_rows[0:UNIT_TILES, :], in_=glu_b1.rearrange("(g p) -> g p", p=P)
+        )
+        nc.scalar.dma_start(
+            out=bias_rows[UNIT_TILES : 2 * UNIT_TILES, :],
+            in_=glu_b2.rearrange("(g p) -> g p", p=P),
+        )
+
+        zero_col = keep.tile([P, 1], F32)
+        nc.vector.memset(zero_col[:], 0.0)
+        table_warm = keep.tile([P, 1], F32)
+        nc.scalar.activation(out=table_warm[:], in_=zero_col[:], func=ACT.Sigmoid)
+
+        dt_f32 = keep.tile([P, 1], F32)
+        nc.vector.tensor_copy(out=dt_f32[:], in_=dt_bf16[:])
+
+        ident_bf16 = keep.tile([P, P], BF16)
+        make_identity(nc, ident_bf16[:])
+        ident_f32 = keep.tile([P, P], F32)
+        make_identity(nc, ident_f32[:])
+
+        y_view = y_tilde.rearrange("(p t) k -> p t k", t=ROW_TILES)
+        z_view = z_next.rearrange("(p t) k -> p t k", t=ROW_TILES)
+        out_view = out.rearrange("(p t) g -> p t g", t=ROW_TILES)
+        y_raw = keep.tile([P, ROW_TILES, K], BF16)
+        z_raw = keep.tile([P, ROW_TILES, K], BF16)
+        for t in range(CHUNK_TILES):
+            nc.sync.dma_start(out=y_raw[:, t, :], in_=y_view[:, t, :])
+            nc.sync.dma_start(out=z_raw[:, t, :], in_=z_view[:, t, :])
+        weights = (glu_w1, glu_w2)
+        w_raw = {}
+        for g in range(UNIT_TILES):
+            for w in range(2):
+                w_raw[w, g] = keep.tile([P, K], BF16, name="w_raw_%d_%d" % (w, g))
+                nc.sync.dma_start(out=w_raw[w, g][:], in_=weights[w][g * P : (g + 1) * P, :])
+        for c in range(1, CHUNKS):
+            tiles = slice(c * CHUNK_TILES, (c + 1) * CHUNK_TILES)
+            nc.sync.dma_start(out=y_raw[:, tiles, :], in_=y_view[:, tiles, :])
+            nc.sync.dma_start(out=z_raw[:, tiles, :], in_=z_view[:, tiles, :])
+
+        y_codes = keep.tile([P, PASSES, ROWS], U32, align_bytes=64)
+        y_scales = keep.tile([P, PASSES, ROWS], U8, align_bytes=64)
+        w_codes = keep.tile([P, 2, UNIT_TILES, PASSES * P], U32, align_bytes=64)
+        w_scales = keep.tile([P, 2, UNIT_TILES, PASSES * P], U8, align_bytes=64)
+        bias_cols = keep.tile([P, 2 * UNIT_TILES], F32)
+        out_rows = keep.tile([P, ROW_TILES, UNITS], F32)
+
+        y_next = {}
+        y_grouped = {}
+        w_grouped = {}
+        acc = {}
+        gate = {}
+        gated = {}
+        flipped_out = {}
+
+        def update_rows(t):
+            y_next[t] = rows_pool.tile([P, 2, K // 2], BF16, name="y_next", tag="y_next")
+            nc.vector.scalar_tensor_tensor(
+                out=y_next[t][:],
+                in0=z_raw[:, t, :].rearrange("p (i e) -> p e i", e=2),
+                scalar=dt_f32[:, 0:1],
+                in1=y_raw[:, t, :].rearrange("p (i e) -> p e i", e=2),
+                op0=ALU.mult,
+                op1=ALU.add,
+            )
+
+        def transpose_rows(t):
+            flipped = flip_in_pool.tile([P, PASSES * PACK, P], BF16, name="flipped_in", tag="flipped_in")
+            for s in range(PASSES):
+                for u in range(2):
+                    for e in range(2):
+                        first = (2 * s + u) * P
+                        nc.tensor.transpose(
+                            flipped[:, PACK * s + 2 * u + e, :],
+                            y_next[t][:, e, first : first + P],
+                            ident_bf16[:],
+                        )
+            y_grouped[t] = grouped_pool.tile(
+                [P, PASSES, P, PACK], BF16, name="y_grouped", tag="y_grouped", align_bytes=64
+            )
+            nc.scalar.copy(
+                out=y_grouped[t][:],
+                in_=flipped[:].rearrange("p (s j) r -> p s r j", s=PASSES),
+            )
+
+        def quantise_rows(t):
+            cols = slice(t * P, (t + 1) * P)
+            for s in range(PASSES):
+                nc.vector.quantize_mx(
+                    out=y_codes[:, s, cols].bitcast(FP8X4),
+                    scales=y_scales[:, s, cols],
+                    in_=y_grouped[t][:, s, :, :].rearrange("p r j -> p (r j)"),
+                )
+
+        def transpose_weights(w, g):
+            words = w_raw[w, g][:].bitcast(F32)
+            flipped = flip_in_pool.tile([P, PASSES * 2, P], F32, name="flipped_in", tag="flipped_in")
+            for c in range(PASSES * 2):
+                nc.tensor.transpose(flipped[:, c, :], words[:, c * P : (c + 1) * P], ident_f32[:])
+            w_grouped[w, g] = grouped_pool.tile([P, PASSES * P * PACK], BF16, name="w_grouped", tag="w_grouped", align_bytes=64)
+            nc.scalar.copy(
+                out=w_grouped[w, g][:].bitcast(F32).rearrange("p (s m u) -> p s m u", s=PASSES, u=2),
+                in_=flipped[:].rearrange("p (s u) m -> p s m u", u=2),
+            )
+
+        def quantise_weights(w, g):
+            nc.vector.quantize_mx(
+                out=w_codes[:, w, g, :].bitcast(FP8X4),
+                scales=w_scales[:, w, g, :],
+                in_=w_grouped[w, g][:],
+            )
+
+        def chunk_and_units(step):
+            return divmod(step, UNIT_TILES)
+
+        def multiply(step):
+            c, g = chunk_and_units(step)
+            cols = slice(c * CHUNK, (c + 1) * CHUNK)
+            for w in range(2):
+                acc[w, step] = acc_pool.tile([P, CHUNK], F32, name="acc_%d" % w, tag="acc_%d" % w)
+                for s in range(PASSES):
+                    units = slice(s * P, (s + 1) * P)
+                    nc.tensor.matmul_mx(
+                        out=acc[w, step][:],
+                        lhsT=w_codes[:, w, g, units].bitcast(FP8X4),
+                        lhsT_scale=w_scales[:, w, g, units],
+                        rhs=y_codes[:, s, cols].bitcast(FP8X4),
+                        rhs_scale=y_scales[:, s, cols],
+                        start=(s == 0),
+                        stop=(s == PASSES - 1),
+                    )
+
+        def open_gate(step):
+            c, g = chunk_and_units(step)
+            gate[step] = gated_pool.tile([P, CHUNK], F32, name="gate", tag="gate")
+            nc.scalar.activation(
+                out=gate[step][:],
+                in_=acc[0, step][:],
+                func=ACT.Sigmoid,
+                bias=bias_cols[:, g : g + 1],
+                scale=1.0,
+            )
+
+        def apply_gate(step):
+            c, g = chunk_and_units(step)
+            gated[step] = gated_pool.tile([P, CHUNK], F32, name="gated", tag="gated")
+            nc.vector.scalar_tensor_tensor(
+                out=gated[step][:],
+                in0=acc[1, step][:],
+                scalar=bias_cols[:, UNIT_TILES + g : UNIT_TILES + g + 1],
+                in1=gate[step][:],
+                op0=ALU.add,
+                op1=ALU.mult,
+            )
+
+        def transpose_out(step):
+            flipped_out[step] = flip_out_pool.tile([P, CHUNK_TILES, P], F32, name="flipped_out", tag="flipped_out")
+            for t in range(CHUNK_TILES):
+                nc.tensor.transpose(
+                    flipped_out[step][:, t, :], gated[step][:, t * P : (t + 1) * P], ident_f32[:]
+                )
+
+        def copy_out(step):
+            c, g = chunk_and_units(step)
+            tiles = slice(c * CHUNK_TILES, (c + 1) * CHUNK_TILES)
+            target = out_rows[:, tiles, g * P : (g + 1) * P]
+            if c == 0:
+                nc.vector.tensor_copy(out=target, in_=flipped_out[step][:])
+            else:
+                nc.scalar.copy(out=target, in_=flipped_out[step][:])
+            if g % STORE_TILES == STORE_TILES - 1:
+                units = slice((g + 1 - STORE_TILES) * P, (g + 1) * P)
+                nc.sync.dma_start(out=out_view[:, tiles, units], in_=out_rows[:, tiles, units])
+
+        ITEMS = UNIT_TILES + (ROW_TILES - CHUNK_TILES) // 2
+
+        def row_tiles_of(item):
+            first = CHUNK_TILES + 2 * (item - UNIT_TILES)
+            return (first, first + 1)
+
+        def prepare_update(item):
+            if UNIT_TILES <= item < ITEMS:
+                for t in row_tiles_of(item):
+                    update_rows(t)
+
+        def prepare_transpose(item):
+            if item < UNIT_TILES:
+                for w in range(2):
+                    transpose_weights(w, item)
+            elif item < ITEMS:
+                for t in row_tiles_of(item):
+                    transpose_rows(t)
+
+        def prepare_quantise(item):
+            if item < UNIT_TILES:
+                for w in range(2):
+                    quantise_weights(w, item)
+            elif item < ITEMS:
+                for t in row_tiles_of(item):
+                    quantise_rows(t)
+
+        update_rows(0)
+        for t in range(CHUNK_TILES):
+            if t + 1 < CHUNK_TILES:
+                update_rows(t + 1)
+            transpose_rows(t)
+            if t >= 1:
+                quantise_rows(t - 1)
+        quantise_rows(CHUNK_TILES - 1)
+
+        bias_flipped = flip_in_pool.tile([P, P], BF16, name="flipped_in", tag="flipped_in")
+        nc.tensor.transpose(bias_flipped[:], bias_rows[:], ident_bf16[:])
+        nc.vector.tensor_copy(out=bias_cols[:], in_=bias_flipped[:, 0 : 2 * UNIT_TILES])
+
+        prepare_transpose(0)
+        prepare_transpose(1)
+        prepare_quantise(0)
+
+        for step in range(STEPS + 2):
+            prepare_quantise(step + 1)
+            if 1 <= step <= STEPS:
+                apply_gate(step - 1)
+            if step >= 2:
+                copy_out(step - 2)
+            prepare_transpose(step + 2)
+            prepare_update(step + 3)
+            if step < STEPS:
+                multiply(step)
+                open_gate(step)
+            if 1 <= step <= STEPS:
+                transpose_out(step - 1)

@@ -16,7 +16,8 @@ ROWS = 1024
 K = 1024
 UNITS = 1024
 PACK = 4
-PASSES = K // (P * PACK)
+K_PASS = P * PACK
+PASSES = K // K_PASS
 ROW_TILES = ROWS // P
 UNIT_TILES = UNITS // P
 CHUNK_TILES = 4
@@ -39,8 +40,7 @@ def tile_instrumentedlocmblock_pb_kernel(
         grouped_pool = ctx.enter_context(tc.tile_pool(name="grouped", bufs=4))
         gated_pool = ctx.enter_context(tc.tile_pool(name="gated", bufs=3))
         acc_pool = ctx.enter_context(tc.psum_pool(name="acc", bufs=2))
-        flip_in_pool = ctx.enter_context(tc.psum_pool(name="flip_in", bufs=2))
-        flip_out_pool = ctx.enter_context(tc.psum_pool(name="flip_out", bufs=2))
+        flip_pool = ctx.enter_context(tc.psum_pool(name="flip", bufs=4))
 
         dt_bf16 = keep.tile([P, 1], BF16)
         nc.scalar.dma_start(out=dt_bf16[:], in_=dt.partition_broadcast(P))
@@ -82,10 +82,10 @@ def tile_instrumentedlocmblock_pb_kernel(
             for w in range(2):
                 w_raw[w, g] = keep.tile([P, K], BF16, name="w_raw_%d_%d" % (w, g))
                 nc.sync.dma_start(out=w_raw[w, g][:], in_=weights[w][g * P : (g + 1) * P, :])
-        for c in range(1, CHUNKS):
-            tiles = slice(c * CHUNK_TILES, (c + 1) * CHUNK_TILES)
-            nc.sync.dma_start(out=y_raw[:, tiles, :], in_=y_view[:, tiles, :])
-            nc.sync.dma_start(out=z_raw[:, tiles, :], in_=z_view[:, tiles, :])
+            if g % 2 == 0:
+                t = CHUNK_TILES + g // 2
+                nc.sync.dma_start(out=y_raw[:, t, :], in_=y_view[:, t, :])
+                nc.sync.dma_start(out=z_raw[:, t, :], in_=z_view[:, t, :])
 
         y_codes = keep.tile([P, PASSES, ROWS], U32, align_bytes=64)
         y_scales = keep.tile([P, PASSES, ROWS], U8, align_bytes=64)
@@ -102,62 +102,57 @@ def tile_instrumentedlocmblock_pb_kernel(
         gated = {}
         flipped_out = {}
 
-        def update_rows(t):
-            y_next[t] = rows_pool.tile([P, 2, K // 2], BF16, name="y_next", tag="y_next")
+        def regroup(source, grouped, passes):
+            words = source.bitcast(F32)
+            flipped = flip_pool.tile([P, passes * 2, P], F32, name="flipped", tag="flipped")
+            for c in range(passes * 2):
+                nc.tensor.transpose(flipped[:, c, :], words[:, c * P : (c + 1) * P], ident_f32[:])
+            nc.scalar.copy(
+                out=grouped.bitcast(F32).rearrange("p (s r u) -> p s r u", s=passes, u=2),
+                in_=flipped[:].rearrange("p (s u) r -> p s r u", u=2),
+            )
+
+        def update_rows(t, first, count):
+            ks = slice(first * K_PASS, (first + count) * K_PASS)
+            y_next[t, first] = rows_pool.tile([P, count * K_PASS], BF16, name="y_next", tag="y_next")
             nc.vector.scalar_tensor_tensor(
-                out=y_next[t][:],
-                in0=z_raw[:, t, :].rearrange("p (i e) -> p e i", e=2),
+                out=y_next[t, first][:],
+                in0=z_raw[:, t, ks],
                 scalar=dt_f32[:, 0:1],
-                in1=y_raw[:, t, :].rearrange("p (i e) -> p e i", e=2),
+                in1=y_raw[:, t, ks],
                 op0=ALU.mult,
                 op1=ALU.add,
             )
 
-        def transpose_rows(t):
-            flipped = flip_in_pool.tile([P, PASSES * PACK, P], BF16, name="flipped_in", tag="flipped_in")
-            for s in range(PASSES):
-                for u in range(2):
-                    for e in range(2):
-                        first = (2 * s + u) * P
-                        nc.tensor.transpose(
-                            flipped[:, PACK * s + 2 * u + e, :],
-                            y_next[t][:, e, first : first + P],
-                            ident_bf16[:],
-                        )
-            y_grouped[t] = grouped_pool.tile(
-                [P, PASSES, P, PACK], BF16, name="y_grouped", tag="y_grouped", align_bytes=64
+        def transpose_rows(t, first, count):
+            y_grouped[t, first] = grouped_pool.tile(
+                [P, count * K_PASS], BF16, name="y_grouped", tag="y_grouped", align_bytes=64
             )
-            nc.scalar.copy(
-                out=y_grouped[t][:],
-                in_=flipped[:].rearrange("p (s j) r -> p s r j", s=PASSES),
-            )
+            regroup(y_next[t, first][:], y_grouped[t, first][:], count)
 
-        def quantise_rows(t):
+        def quantise_rows(t, first, count):
             cols = slice(t * P, (t + 1) * P)
-            for s in range(PASSES):
+            for i in range(count):
                 nc.vector.quantize_mx(
-                    out=y_codes[:, s, cols].bitcast(FP8X4),
-                    scales=y_scales[:, s, cols],
-                    in_=y_grouped[t][:, s, :, :].rearrange("p r j -> p (r j)"),
+                    out=y_codes[:, first + i, cols].bitcast(FP8X4),
+                    scales=y_scales[:, first + i, cols],
+                    in_=y_grouped[t, first][:, i * K_PASS : (i + 1) * K_PASS],
                 )
 
-        def transpose_weights(w, g):
-            words = w_raw[w, g][:].bitcast(F32)
-            flipped = flip_in_pool.tile([P, PASSES * 2, P], F32, name="flipped_in", tag="flipped_in")
-            for c in range(PASSES * 2):
-                nc.tensor.transpose(flipped[:, c, :], words[:, c * P : (c + 1) * P], ident_f32[:])
-            w_grouped[w, g] = grouped_pool.tile([P, PASSES * P * PACK], BF16, name="w_grouped", tag="w_grouped", align_bytes=64)
-            nc.scalar.copy(
-                out=w_grouped[w, g][:].bitcast(F32).rearrange("p (s m u) -> p s m u", s=PASSES, u=2),
-                in_=flipped[:].rearrange("p (s u) m -> p s m u", u=2),
-            )
+        def transpose_weights(g):
+            for w in range(2):
+                w_grouped[w, g] = grouped_pool.tile(
+                    [P, K], BF16, name="w_grouped", tag="w_grouped", align_bytes=64
+                )
+                regroup(w_raw[w, g][:], w_grouped[w, g][:], PASSES)
 
-        def quantise_weights(w, g):
-            nc.vector.quantize_mx(
-                out=w_codes[:, w, g, :].bitcast(FP8X4),
-                scales=w_scales[:, w, g, :],
-                in_=w_grouped[w, g][:],
-            )
+        def quantise_weights(g):
+            for w in range(2):
+                nc.vector.quantize_mx(
+                    out=w_codes[:, w, g, :].bitcast(FP8X4),
+                    scales=w_scales[:, w, g, :],
+                    in_=w_grouped[w, g][:],
+                )
 
         def chunk_and_units(step):
             return divmod(step, UNIT_TILES)
@@ -203,7 +198,7 @@ def tile_instrumentedlocmblock_pb_kernel(
             )
 
         def transpose_out(step):
-            flipped_out[step] = flip_out_pool.tile([P, CHUNK_TILES, P], F32, name="flipped_out", tag="flipped_out")
+            flipped_out[step] = flip_pool.tile([P, CHUNK_TILES, P], F32, name="flipped", tag="flipped")
             for t in range(CHUNK_TILES):
                 nc.tensor.transpose(
                     flipped_out[step][:, t, :], gated[step][:, t * P : (t + 1) * P], ident_f32[:]
@@ -212,69 +207,54 @@ def tile_instrumentedlocmblock_pb_kernel(
         def copy_out(step):
             c, g = chunk_and_units(step)
             tiles = slice(c * CHUNK_TILES, (c + 1) * CHUNK_TILES)
-            target = out_rows[:, tiles, g * P : (g + 1) * P]
-            if c == 0:
-                nc.vector.tensor_copy(out=target, in_=flipped_out[step][:])
-            else:
-                nc.scalar.copy(out=target, in_=flipped_out[step][:])
+            copy = nc.vector.tensor_copy if step % 2 == 0 else nc.scalar.copy
+            copy(out=out_rows[:, tiles, g * P : (g + 1) * P], in_=flipped_out[step][:])
             if g % STORE_TILES == STORE_TILES - 1:
                 units = slice((g + 1 - STORE_TILES) * P, (g + 1) * P)
                 nc.sync.dma_start(out=out_view[:, tiles, units], in_=out_rows[:, tiles, units])
 
-        ITEMS = UNIT_TILES + (ROW_TILES - CHUNK_TILES) // 2
-
-        def row_tiles_of(item):
-            first = CHUNK_TILES + 2 * (item - UNIT_TILES)
-            return (first, first + 1)
-
-        def prepare_update(item):
-            if UNIT_TILES <= item < ITEMS:
-                for t in row_tiles_of(item):
-                    update_rows(t)
-
-        def prepare_transpose(item):
-            if item < UNIT_TILES:
-                for w in range(2):
-                    transpose_weights(w, item)
-            elif item < ITEMS:
-                for t in row_tiles_of(item):
-                    transpose_rows(t)
-
-        def prepare_quantise(item):
-            if item < UNIT_TILES:
-                for w in range(2):
-                    quantise_weights(w, item)
-            elif item < ITEMS:
-                for t in row_tiles_of(item):
-                    quantise_rows(t)
-
-        update_rows(0)
+        update_rows(0, 0, PASSES)
         for t in range(CHUNK_TILES):
             if t + 1 < CHUNK_TILES:
-                update_rows(t + 1)
-            transpose_rows(t)
-            if t >= 1:
-                quantise_rows(t - 1)
-        quantise_rows(CHUNK_TILES - 1)
+                update_rows(t + 1, 0, PASSES)
+            transpose_rows(t, 0, PASSES)
+        for t in range(CHUNK_TILES):
+            quantise_rows(t, 0, PASSES)
 
-        bias_flipped = flip_in_pool.tile([P, P], BF16, name="flipped_in", tag="flipped_in")
+        LATER = (ROW_TILES - CHUNK_TILES) * PASSES
+
+        def later_piece(j):
+            t, first = divmod(j, PASSES)
+            return CHUNK_TILES + t, first, 1
+
+        update_rows(*later_piece(0))
+        transpose_weights(0)
+        quantise_weights(0)
+
+        bias_flipped = flip_pool.tile([P, P], BF16, name="flipped", tag="flipped")
         nc.tensor.transpose(bias_flipped[:], bias_rows[:], ident_bf16[:])
         nc.vector.tensor_copy(out=bias_cols[:], in_=bias_flipped[:, 0 : 2 * UNIT_TILES])
 
-        prepare_transpose(0)
-        prepare_transpose(1)
-        prepare_quantise(0)
+        transpose_weights(1)
+        transpose_rows(*later_piece(0))
 
-        for step in range(STEPS + 2):
-            prepare_quantise(step + 1)
-            if 1 <= step <= STEPS:
-                apply_gate(step - 1)
-            if step >= 2:
-                copy_out(step - 2)
-            prepare_transpose(step + 2)
-            prepare_update(step + 3)
+        for step in range(STEPS + 1):
             if step < STEPS:
                 multiply(step)
                 open_gate(step)
-            if 1 <= step <= STEPS:
+            if step + 1 < LATER:
+                update_rows(*later_piece(step + 1))
+            if step + 1 < UNIT_TILES:
+                quantise_weights(step + 1)
+            if step < LATER:
+                quantise_rows(*later_piece(step))
+            if step >= 1:
                 transpose_out(step - 1)
+            if step < STEPS:
+                apply_gate(step)
+            if step >= 1:
+                copy_out(step - 1)
+            if step + 2 < UNIT_TILES:
+                transpose_weights(step + 2)
+            if step + 1 < LATER:
+                transpose_rows(*later_piece(step + 1))

@@ -18,12 +18,10 @@ UNITS = 1024
 PACK = 4
 K_PASS = P * PACK
 PASSES = K // K_PASS
+BANK = 512
 ROW_TILES = ROWS // P
 UNIT_TILES = UNITS // P
-CHUNK_TILES = 4
-CHUNK = CHUNK_TILES * P
-CHUNKS = ROW_TILES // CHUNK_TILES
-STEPS = CHUNKS * UNIT_TILES
+FIRST_TILES = BANK // P
 STORE_TILES = 2
 
 FLOPS = 2 * 2 * ROWS * K * UNITS
@@ -73,9 +71,13 @@ def tile_instrumentedlocmblock_pb_kernel(
         out_view = out.rearrange("(p t) g -> p t g", t=ROW_TILES)
         y_raw = keep.tile([P, ROW_TILES, K], BF16)
         z_raw = keep.tile([P, ROW_TILES, K], BF16)
-        for t in range(CHUNK_TILES):
+
+        def load_rows(t):
             nc.sync.dma_start(out=y_raw[:, t, :], in_=y_view[:, t, :])
             nc.sync.dma_start(out=z_raw[:, t, :], in_=z_view[:, t, :])
+
+        for t in range(FIRST_TILES):
+            load_rows(t)
         weights = (glu_w1, glu_w2)
         w_raw = {}
         for g in range(UNIT_TILES):
@@ -83,14 +85,15 @@ def tile_instrumentedlocmblock_pb_kernel(
                 w_raw[w, g] = keep.tile([P, K], BF16, name="w_raw_%d_%d" % (w, g))
                 nc.sync.dma_start(out=w_raw[w, g][:], in_=weights[w][g * P : (g + 1) * P, :])
             if g % 2 == 0:
-                t = CHUNK_TILES + g // 2
-                nc.sync.dma_start(out=y_raw[:, t, :], in_=y_view[:, t, :])
-                nc.sync.dma_start(out=z_raw[:, t, :], in_=z_view[:, t, :])
+                load_rows(FIRST_TILES + g // 2)
+        bias_all = keep.tile([P, 2, UNITS], BF16)
+        nc.sync.dma_start(out=bias_all[:, 0, :], in_=glu_b1.partition_broadcast(P))
+        nc.sync.dma_start(out=bias_all[:, 1, :], in_=glu_b2.partition_broadcast(P))
 
         y_codes = keep.tile([P, PASSES, ROWS], U32, align_bytes=64)
         y_scales = keep.tile([P, PASSES, ROWS], U8, align_bytes=64)
-        w_codes = keep.tile([P, 2, UNIT_TILES, PASSES * P], U32, align_bytes=64)
-        w_scales = keep.tile([P, 2, UNIT_TILES, PASSES * P], U8, align_bytes=64)
+        w_codes = keep.tile([P, 2, PASSES, UNITS], U32, align_bytes=64)
+        w_scales = keep.tile([P, 2, PASSES, UNITS], U8, align_bytes=64)
         bias_cols = keep.tile([P, 2 * UNIT_TILES], F32)
         out_rows = keep.tile([P, ROW_TILES, UNITS], F32)
 
@@ -112,6 +115,14 @@ def tile_instrumentedlocmblock_pb_kernel(
                 in_=flipped[:].rearrange("p (s u) r -> p s r u", u=2),
             )
 
+        def quantise(grouped, codes, scales, first, count, cols):
+            for i in range(count):
+                nc.vector.quantize_mx(
+                    out=codes[:, first + i, cols].bitcast(FP8X4),
+                    scales=scales[:, first + i, cols],
+                    in_=grouped[:, i * K_PASS : (i + 1) * K_PASS],
+                )
+
         def update_rows(t, first, count):
             ks = slice(first * K_PASS, (first + count) * K_PASS)
             y_next[t, first] = rows_pool.tile([P, count * K_PASS], BF16, name="y_next", tag="y_next")
@@ -131,13 +142,7 @@ def tile_instrumentedlocmblock_pb_kernel(
             regroup(y_next[t, first][:], y_grouped[t, first][:], count)
 
         def quantise_rows(t, first, count):
-            cols = slice(t * P, (t + 1) * P)
-            for i in range(count):
-                nc.vector.quantize_mx(
-                    out=y_codes[:, first + i, cols].bitcast(FP8X4),
-                    scales=y_scales[:, first + i, cols],
-                    in_=y_grouped[t, first][:, i * K_PASS : (i + 1) * K_PASS],
-                )
+            quantise(y_grouped[t, first], y_codes, y_scales, first, count, slice(t * P, (t + 1) * P))
 
         def transpose_weights(g):
             for w in range(2):
@@ -148,84 +153,109 @@ def tile_instrumentedlocmblock_pb_kernel(
 
         def quantise_weights(g):
             for w in range(2):
-                nc.vector.quantize_mx(
-                    out=w_codes[:, w, g, :].bitcast(FP8X4),
-                    scales=w_scales[:, w, g, :],
-                    in_=w_grouped[w, g][:],
+                quantise(
+                    w_grouped[w, g],
+                    w_codes[:, w, :, :],
+                    w_scales[:, w, :, :],
+                    0,
+                    PASSES,
+                    slice(g * P, (g + 1) * P),
                 )
 
-        def chunk_and_units(step):
-            return divmod(step, UNIT_TILES)
+        def rows_operand(rows):
+            return lambda w, s: (y_codes[:, s, rows], y_scales[:, s, rows])
 
-        def multiply(step):
-            c, g = chunk_and_units(step)
-            cols = slice(c * CHUNK, (c + 1) * CHUNK)
+        def units_operand(units):
+            return lambda w, s: (w_codes[:, w, s, units], w_scales[:, w, s, units])
+
+        def multiply(stationary, moving):
+            sums = []
             for w in range(2):
-                acc[w, step] = acc_pool.tile([P, CHUNK], F32, name="acc_%d" % w, tag="acc_%d" % w)
+                total = acc_pool.tile([P, BANK], F32, name="acc_%d" % w, tag="acc_%d" % w)
                 for s in range(PASSES):
-                    units = slice(s * P, (s + 1) * P)
+                    lhs_codes, lhs_scales = stationary(w, s)
+                    rhs_codes, rhs_scales = moving(w, s)
                     nc.tensor.matmul_mx(
-                        out=acc[w, step][:],
-                        lhsT=w_codes[:, w, g, units].bitcast(FP8X4),
-                        lhsT_scale=w_scales[:, w, g, units],
-                        rhs=y_codes[:, s, cols].bitcast(FP8X4),
-                        rhs_scale=y_scales[:, s, cols],
+                        out=total[:],
+                        lhsT=lhs_codes.bitcast(FP8X4),
+                        lhsT_scale=lhs_scales,
+                        rhs=rhs_codes.bitcast(FP8X4),
+                        rhs_scale=rhs_scales,
                         start=(s == 0),
                         stop=(s == PASSES - 1),
                     )
+                sums.append(total)
+            return sums
 
-        def open_gate(step):
-            c, g = chunk_and_units(step)
-            gate[step] = gated_pool.tile([P, CHUNK], F32, name="gate", tag="gate")
+        def multiply_units(g):
+            acc[g] = multiply(units_operand(slice(g * P, (g + 1) * P)), rows_operand(slice(0, BANK)))
+
+        def open_gate(g):
+            gate[g] = gated_pool.tile([P, BANK], F32, name="gate", tag="gate")
             nc.scalar.activation(
-                out=gate[step][:],
-                in_=acc[0, step][:],
+                out=gate[g][:],
+                in_=acc[g][0][:],
                 func=ACT.Sigmoid,
                 bias=bias_cols[:, g : g + 1],
                 scale=1.0,
             )
 
-        def apply_gate(step):
-            c, g = chunk_and_units(step)
-            gated[step] = gated_pool.tile([P, CHUNK], F32, name="gated", tag="gated")
+        def apply_gate(g):
+            gated[g] = gated_pool.tile([P, BANK], F32, name="gated", tag="gated")
             nc.vector.scalar_tensor_tensor(
-                out=gated[step][:],
-                in0=acc[1, step][:],
+                out=gated[g][:],
+                in0=acc[g][1][:],
                 scalar=bias_cols[:, UNIT_TILES + g : UNIT_TILES + g + 1],
-                in1=gate[step][:],
+                in1=gate[g][:],
                 op0=ALU.add,
                 op1=ALU.mult,
             )
 
-        def transpose_out(step):
-            flipped_out[step] = flip_pool.tile([P, CHUNK_TILES, P], F32, name="flipped", tag="flipped")
-            for t in range(CHUNK_TILES):
+        def transpose_out(g):
+            flipped_out[g] = flip_pool.tile([P, FIRST_TILES, P], F32, name="flipped", tag="flipped")
+            for t in range(FIRST_TILES):
                 nc.tensor.transpose(
-                    flipped_out[step][:, t, :], gated[step][:, t * P : (t + 1) * P], ident_f32[:]
+                    flipped_out[g][:, t, :], gated[g][:, t * P : (t + 1) * P], ident_f32[:]
                 )
 
-        def copy_out(step):
-            c, g = chunk_and_units(step)
-            tiles = slice(c * CHUNK_TILES, (c + 1) * CHUNK_TILES)
-            copy = nc.vector.tensor_copy if step % 2 == 0 else nc.scalar.copy
-            copy(out=out_rows[:, tiles, g * P : (g + 1) * P], in_=flipped_out[step][:])
+        def copy_out(g):
+            copy = nc.vector.tensor_copy if g % 2 == 0 else nc.scalar.copy
+            copy(out=out_rows[:, 0:FIRST_TILES, g * P : (g + 1) * P], in_=flipped_out[g][:])
             if g % STORE_TILES == STORE_TILES - 1:
                 units = slice((g + 1 - STORE_TILES) * P, (g + 1) * P)
-                nc.sync.dma_start(out=out_view[:, tiles, units], in_=out_rows[:, tiles, units])
+                nc.sync.dma_start(
+                    out=out_view[:, 0:FIRST_TILES, units], in_=out_rows[:, 0:FIRST_TILES, units]
+                )
+
+        def rows_step(t, half):
+            units = slice(half * BANK, (half + 1) * BANK)
+            sums = multiply(rows_operand(slice(t * P, (t + 1) * P)), units_operand(units))
+            biased = []
+            for w in range(2):
+                biased.append(gated_pool.tile([P, BANK], F32, name="biased_%d" % w, tag="biased_%d" % w))
+                nc.vector.tensor_tensor(
+                    out=biased[w][:], in0=sums[w][:], in1=bias_all[:, w, units], op=ALU.add
+                )
+            gate_rows = gated_pool.tile([P, BANK], F32, name="gate", tag="gate")
+            nc.scalar.activation(out=gate_rows[:], in_=biased[0][:], func=ACT.Sigmoid)
+            nc.gpsimd.tensor_tensor(
+                out=out_rows[:, t, units], in0=gate_rows[:], in1=biased[1][:], op=ALU.mult
+            )
+            nc.sync.dma_start(out=out_view[:, t, units], in_=out_rows[:, t, units])
 
         update_rows(0, 0, PASSES)
-        for t in range(CHUNK_TILES):
-            if t + 1 < CHUNK_TILES:
+        for t in range(FIRST_TILES):
+            if t + 1 < FIRST_TILES:
                 update_rows(t + 1, 0, PASSES)
             transpose_rows(t, 0, PASSES)
-        for t in range(CHUNK_TILES):
+        for t in range(FIRST_TILES):
             quantise_rows(t, 0, PASSES)
 
-        LATER = (ROW_TILES - CHUNK_TILES) * PASSES
+        LATER = (ROW_TILES - FIRST_TILES) * PASSES
 
         def later_piece(j):
             t, first = divmod(j, PASSES)
-            return CHUNK_TILES + t, first, 1
+            return FIRST_TILES + t, first, 1
 
         update_rows(*later_piece(0))
         transpose_weights(0)
@@ -238,23 +268,27 @@ def tile_instrumentedlocmblock_pb_kernel(
         transpose_weights(1)
         transpose_rows(*later_piece(0))
 
-        for step in range(STEPS + 1):
-            if step < STEPS:
-                multiply(step)
-                open_gate(step)
-            if step + 1 < LATER:
-                update_rows(*later_piece(step + 1))
-            if step + 1 < UNIT_TILES:
-                quantise_weights(step + 1)
-            if step < LATER:
-                quantise_rows(*later_piece(step))
-            if step >= 1:
-                transpose_out(step - 1)
-            if step < STEPS:
-                apply_gate(step)
-            if step >= 1:
-                copy_out(step - 1)
-            if step + 2 < UNIT_TILES:
-                transpose_weights(step + 2)
-            if step + 1 < LATER:
-                transpose_rows(*later_piece(step + 1))
+        for g in range(UNIT_TILES):
+            multiply_units(g)
+            open_gate(g)
+            if g + 1 < LATER:
+                update_rows(*later_piece(g + 1))
+            if g + 1 < UNIT_TILES:
+                quantise_weights(g + 1)
+            quantise_rows(*later_piece(g))
+            if g >= 1:
+                transpose_out(g - 1)
+            apply_gate(g)
+            if g >= 1:
+                copy_out(g - 1)
+            if g + 2 < UNIT_TILES:
+                transpose_weights(g + 2)
+            if g + 1 < LATER:
+                transpose_rows(*later_piece(g + 1))
+
+        later_steps = [(t, half) for t in range(FIRST_TILES, ROW_TILES) for half in range(UNITS // BANK)]
+        rows_step(*later_steps[0])
+        transpose_out(UNIT_TILES - 1)
+        copy_out(UNIT_TILES - 1)
+        for t, half in later_steps[1:]:
+            rows_step(t, half)

from contextlib import ExitStack

import concourse.mybir as mybir
from concourse.masks import make_identity

F32 = mybir.dt.float32
BF16 = mybir.dt.bfloat16
U32 = mybir.dt.uint32
U8 = mybir.dt.uint8
FP8X4 = mybir.dt.float8_e4m3fn_x4
ALU = mybir.AluOpType
ACT = mybir.ActivationFunctionType

P = 128
ROWS = 1024
K = 1024
UNITS = 1024
PACK = 4
K_PASS = P * PACK
PASSES = K // K_PASS
BANK = 512
ROW_TILES = ROWS // P
UNIT_TILES = UNITS // P
FIRST_TILES = BANK // P
STORE_TILES = 2

FLOPS = 2 * 2 * ROWS * K * UNITS


def tile_instrumentedlocmblock_pb_kernel(
    tc, y_tilde, z_next, dt, glu_w1, glu_w2, glu_b1, glu_b2, out
):
    nc = tc.nc
    with ExitStack() as ctx:
        ctx.enter_context(tc.manual_schedule())
        keep = ctx.enter_context(tc.tile_pool(name="keep", bufs=1))
        rows_pool = ctx.enter_context(tc.tile_pool(name="rows", bufs=4))
        grouped_pool = ctx.enter_context(tc.tile_pool(name="grouped", bufs=4))
        gated_pool = ctx.enter_context(tc.tile_pool(name="gated", bufs=3))
        acc_pool = ctx.enter_context(tc.psum_pool(name="acc", bufs=2))
        flip_pool = ctx.enter_context(tc.psum_pool(name="flip", bufs=4))

        dt_bf16 = keep.tile([P, 1], BF16)
        nc.scalar.dma_start(out=dt_bf16[:], in_=dt.partition_broadcast(P))

        bias_rows = keep.tile([P, P], BF16)
        nc.vector.memset(bias_rows[:], 0.0)
        nc.scalar.dma_start(
            out=bias_rows[0:UNIT_TILES, :], in_=glu_b1.rearrange("(g p) -> g p", p=P)
        )
        nc.scalar.dma_start(
            out=bias_rows[UNIT_TILES : 2 * UNIT_TILES, :],
            in_=glu_b2.rearrange("(g p) -> g p", p=P),
        )

        zero_col = keep.tile([P, 1], F32)
        nc.vector.memset(zero_col[:], 0.0)
        table_warm = keep.tile([P, 1], F32)
        nc.scalar.activation(out=table_warm[:], in_=zero_col[:], func=ACT.Sigmoid)

        dt_f32 = keep.tile([P, 1], F32)
        nc.vector.tensor_copy(out=dt_f32[:], in_=dt_bf16[:])

        ident_bf16 = keep.tile([P, P], BF16)
        make_identity(nc, ident_bf16[:])
        ident_f32 = keep.tile([P, P], F32)
        make_identity(nc, ident_f32[:])

        y_view = y_tilde.rearrange("(p t) k -> p t k", t=ROW_TILES)
        z_view = z_next.rearrange("(p t) k -> p t k", t=ROW_TILES)
        out_view = out.rearrange("(p t) g -> p t g", t=ROW_TILES)
        y_raw = keep.tile([P, ROW_TILES, K], BF16)
        z_raw = keep.tile([P, ROW_TILES, K], BF16)

        def load_rows(t):
            nc.sync.dma_start(out=y_raw[:, t, :], in_=y_view[:, t, :])
            nc.sync.dma_start(out=z_raw[:, t, :], in_=z_view[:, t, :])

        for t in range(FIRST_TILES):
            load_rows(t)
        weights = (glu_w1, glu_w2)
        w_raw = {}
        for g in range(UNIT_TILES):
            for w in range(2):
                w_raw[w, g] = keep.tile([P, K], BF16, name="w_raw_%d_%d" % (w, g))
                nc.sync.dma_start(out=w_raw[w, g][:], in_=weights[w][g * P : (g + 1) * P, :])
            if g % 2 == 0:
                load_rows(FIRST_TILES + g // 2)
        bias_all = keep.tile([P, 2, UNITS], BF16)
        nc.sync.dma_start(out=bias_all[:, 0, :], in_=glu_b1.partition_broadcast(P))
        nc.sync.dma_start(out=bias_all[:, 1, :], in_=glu_b2.partition_broadcast(P))

        y_codes = keep.tile([P, PASSES, ROWS], U32, align_bytes=64)
        y_scales = keep.tile([P, PASSES, ROWS], U8, align_bytes=64)
        w_codes = keep.tile([P, 2, PASSES, UNITS], U32, align_bytes=64)
        w_scales = keep.tile([P, 2, PASSES, UNITS], U8, align_bytes=64)
        bias_cols = keep.tile([P, 2 * UNIT_TILES], F32)
        out_rows = keep.tile([P, ROW_TILES, UNITS], F32)

        y_next = {}
        y_grouped = {}
        w_grouped = {}
        acc = {}
        gate = {}
        gated = {}
        flipped_out = {}

        def regroup(source, grouped, passes):
            words = source.bitcast(F32)
            flipped = flip_pool.tile([P, passes * 2, P], F32, name="flipped", tag="flipped")
            for c in range(passes * 2):
                nc.tensor.transpose(flipped[:, c, :], words[:, c * P : (c + 1) * P], ident_f32[:])
            nc.scalar.copy(
                out=grouped.bitcast(F32).rearrange("p (s r u) -> p s r u", s=passes, u=2),
                in_=flipped[:].rearrange("p (s u) r -> p s r u", u=2),
            )

        def quantise(grouped, codes, scales, first, count, cols):
            for i in range(count):
                nc.vector.quantize_mx(
                    out=codes[:, first + i, cols].bitcast(FP8X4),
                    scales=scales[:, first + i, cols],
                    in_=grouped[:, i * K_PASS : (i + 1) * K_PASS],
                )

        def update_rows(t, first, count):
            ks = slice(first * K_PASS, (first + count) * K_PASS)
            y_next[t, first] = rows_pool.tile([P, count * K_PASS], BF16, name="y_next", tag="y_next")
            nc.vector.scalar_tensor_tensor(
                out=y_next[t, first][:],
                in0=z_raw[:, t, ks],
                scalar=dt_f32[:, 0:1],
                in1=y_raw[:, t, ks],
                op0=ALU.mult,
                op1=ALU.add,
            )

        def transpose_rows(t, first, count):
            y_grouped[t, first] = grouped_pool.tile(
                [P, count * K_PASS], BF16, name="y_grouped", tag="y_grouped", align_bytes=64
            )
            regroup(y_next[t, first][:], y_grouped[t, first][:], count)

        def quantise_rows(t, first, count):
            quantise(y_grouped[t, first], y_codes, y_scales, first, count, slice(t * P, (t + 1) * P))

        def transpose_weights(g):
            for w in range(2):
                w_grouped[w, g] = grouped_pool.tile(
                    [P, K], BF16, name="w_grouped", tag="w_grouped", align_bytes=64
                )
                regroup(w_raw[w, g][:], w_grouped[w, g][:], PASSES)

        def quantise_weights(g):
            for w in range(2):
                quantise(
                    w_grouped[w, g],
                    w_codes[:, w, :, :],
                    w_scales[:, w, :, :],
                    0,
                    PASSES,
                    slice(g * P, (g + 1) * P),
                )

        def rows_operand(rows):
            return lambda w, s: (y_codes[:, s, rows], y_scales[:, s, rows])

        def units_operand(units):
            return lambda w, s: (w_codes[:, w, s, units], w_scales[:, w, s, units])

        def multiply(stationary, moving):
            sums = []
            for w in range(2):
                total = acc_pool.tile([P, BANK], F32, name="acc_%d" % w, tag="acc_%d" % w)
                for s in range(PASSES):
                    lhs_codes, lhs_scales = stationary(w, s)
                    rhs_codes, rhs_scales = moving(w, s)
                    nc.tensor.matmul_mx(
                        out=total[:],
                        lhsT=lhs_codes.bitcast(FP8X4),
                        lhsT_scale=lhs_scales,
                        rhs=rhs_codes.bitcast(FP8X4),
                        rhs_scale=rhs_scales,
                        start=(s == 0),
                        stop=(s == PASSES - 1),
                    )
                sums.append(total)
            return sums

        def multiply_units(g):
            acc[g] = multiply(units_operand(slice(g * P, (g + 1) * P)), rows_operand(slice(0, BANK)))

        def open_gate(g):
            gate[g] = gated_pool.tile([P, BANK], F32, name="gate", tag="gate")
            nc.scalar.activation(
                out=gate[g][:],
                in_=acc[g][0][:],
                func=ACT.Sigmoid,
                bias=bias_cols[:, g : g + 1],
                scale=1.0,
            )

        def apply_gate(g):
            gated[g] = gated_pool.tile([P, BANK], F32, name="gated", tag="gated")
            nc.vector.scalar_tensor_tensor(
                out=gated[g][:],
                in0=acc[g][1][:],
                scalar=bias_cols[:, UNIT_TILES + g : UNIT_TILES + g + 1],
                in1=gate[g][:],
                op0=ALU.add,
                op1=ALU.mult,
            )

        def transpose_out(g):
            flipped_out[g] = flip_pool.tile([P, FIRST_TILES, P], F32, name="flipped", tag="flipped")
            for t in range(FIRST_TILES):
                nc.tensor.transpose(
                    flipped_out[g][:, t, :], gated[g][:, t * P : (t + 1) * P], ident_f32[:]
                )

        def copy_out(g):
            copy = nc.vector.tensor_copy if g % 2 == 0 else nc.scalar.copy
            copy(out=out_rows[:, 0:FIRST_TILES, g * P : (g + 1) * P], in_=flipped_out[g][:])
            if g % STORE_TILES == STORE_TILES - 1:
                units = slice((g + 1 - STORE_TILES) * P, (g + 1) * P)
                nc.sync.dma_start(
                    out=out_view[:, 0:FIRST_TILES, units], in_=out_rows[:, 0:FIRST_TILES, units]
                )

        def rows_step(t, half):
            units = slice(half * BANK, (half + 1) * BANK)
            sums = multiply(rows_operand(slice(t * P, (t + 1) * P)), units_operand(units))
            biased = []
            for w in range(2):
                biased.append(gated_pool.tile([P, BANK], F32, name="biased_%d" % w, tag="biased_%d" % w))
                nc.vector.tensor_tensor(
                    out=biased[w][:], in0=sums[w][:], in1=bias_all[:, w, units], op=ALU.add
                )
            gate_rows = gated_pool.tile([P, BANK], F32, name="gate", tag="gate")
            nc.scalar.activation(out=gate_rows[:], in_=biased[0][:], func=ACT.Sigmoid)
            nc.gpsimd.tensor_tensor(
                out=out_rows[:, t, units], in0=gate_rows[:], in1=biased[1][:], op=ALU.mult
            )
            nc.sync.dma_start(out=out_view[:, t, units], in_=out_rows[:, t, units])

        update_rows(0, 0, PASSES)
        for t in range(FIRST_TILES):
            if t + 1 < FIRST_TILES:
                update_rows(t + 1, 0, PASSES)
            transpose_rows(t, 0, PASSES)
        for t in range(FIRST_TILES):
            quantise_rows(t, 0, PASSES)

        LATER = (ROW_TILES - FIRST_TILES) * PASSES

        def later_piece(j):
            t, first = divmod(j, PASSES)
            return FIRST_TILES + t, first, 1

        update_rows(*later_piece(0))
        transpose_weights(0)
        quantise_weights(0)

        bias_flipped = flip_pool.tile([P, P], BF16, name="flipped", tag="flipped")
        nc.tensor.transpose(bias_flipped[:], bias_rows[:], ident_bf16[:])
        nc.vector.tensor_copy(out=bias_cols[:], in_=bias_flipped[:, 0 : 2 * UNIT_TILES])

        transpose_weights(1)
        transpose_rows(*later_piece(0))

        for g in range(UNIT_TILES):
            multiply_units(g)
            open_gate(g)
            if g + 1 < LATER:
                update_rows(*later_piece(g + 1))
            if g + 1 < UNIT_TILES:
                quantise_weights(g + 1)
            quantise_rows(*later_piece(g))
            if g >= 1:
                transpose_out(g - 1)
            apply_gate(g)
            if g >= 1:
                copy_out(g - 1)
            if g + 2 < UNIT_TILES:
                transpose_weights(g + 2)
            if g + 1 < LATER:
                transpose_rows(*later_piece(g + 1))

        later_steps = [(t, half) for t in range(FIRST_TILES, ROW_TILES) for half in range(UNITS // BANK)]
        rows_step(*later_steps[0])
        transpose_out(UNIT_TILES - 1)
        copy_out(UNIT_TILES - 1)
        for t, half in later_steps[1:]:
            rows_step(t, half)
